import numpy as np
import ml_dtypes


def mxq(x, axis, fmt="e4m3"):
    dtype, down = {"e4m3": (ml_dtypes.float8_e4m3fn, 7), "e5m2": (ml_dtypes.float8_e5m2, 14)}[fmt]
    v = np.moveaxis(np.asarray(x, np.float32).astype(ml_dtypes.bfloat16).astype(np.float64), axis, -1)
    blocks = v.reshape(v.shape[:-1] + (-1, 32))
    amax = np.abs(blocks).max(-1, keepdims=True)
    byte = np.maximum(np.where(amax > 0, np.frexp(amax)[1] - 1 + 127, 0) - down, 1)
    scale = np.exp2(byte - 127.0)
    codes = (blocks / scale).astype(np.float32).astype(dtype).astype(np.float64)
    return np.moveaxis((codes * scale).reshape(v.shape), -1, axis)


WIDE = False


def mx_kscale(k):
    if not WIDE:
        return np.ones(k)
    levels = np.array([10, -10, 5, -5, 0])
    a = np.random.permutation(np.resize(levels, k // 512 * 4)).reshape(k // 512, 4)
    idx = np.arange(k)
    return np.exp2(a[idx // 512, idx % 128 // 32])


BF16 = ml_dtypes.bfloat16


def bf(x):
    return np.asarray(x, np.float32).astype(BF16)


def f64(x):
    return np.asarray(x).astype(np.float64)


E2M1 = np.array([0.0, 0.5, 1.0, 1.5, 2.0, 3.0, 4.0, 6.0, -0.0, -0.5, -1.0, -1.5, -2.0, -3.0, -4.0, -6.0])


def pack_weight(w, fmt):
    k, n = w.shape
    w = f64(bf(w)).reshape(k // 32, 32, n)
    amax = np.abs(w).max(1)
    if fmt == "e4m3":
        byte = np.frexp(amax)[1] - 1 + 127 - 7
    else:
        mant, ex = np.frexp(amax / 6.0)
        byte = np.where(mant > 0.5, ex, ex - 1) + 127
    byte = np.clip(np.where(amax > 0, byte, 1), 1, 254)
    scaled = (w * np.exp2(127.0 - byte)[:, None, :]).reshape(k, n).astype(np.float32)
    by_word = np.ascontiguousarray(scaled.reshape(k // 512, 128, 4, n).transpose(0, 1, 3, 2))
    if fmt == "e4m3":
        words = by_word.astype(ml_dtypes.float8_e4m3fn).view(np.uint8)
    else:
        c = by_word.astype(ml_dtypes.float4_e2m1fn).view(np.uint8) & 0xF
        words = c[..., 0::2] | (c[..., 1::2] << 4)
    return np.ascontiguousarray(words), np.ascontiguousarray(byte.astype(np.uint8).reshape(k // 512, 16, n))


def unpack_weight(words, scales, fmt):
    g, p, n, _ = words.shape
    if fmt == "e4m3":
        vals = np.ascontiguousarray(words).view(ml_dtypes.float8_e4m3fn).astype(np.float64)
    else:
        nib = np.empty((g, p, n, 4), np.uint8)
        nib[..., 0::2] = words & 0xF
        nib[..., 1::2] = words >> 4
        vals = E2M1[nib]
    vals = vals * np.repeat(np.exp2(scales.astype(np.float64) - 127.0), 8, axis=1)[..., None]
    return vals.transpose(0, 1, 3, 2).reshape(g * 512, n)


B, P_DIM, H_DIM, X_DIM = 128, 2048, 1024, 2048
FMT = "e4m3"


def sigmoid(v):
    return 1.0 / (1.0 + np.exp(-v))


def setup_inputs():
    sp, sh, sx = mx_kscale(P_DIM), mx_kscale(H_DIM), mx_kscale(X_DIM)

    def lin_w(in_d, s):
        w = np.random.standard_normal((H_DIM, in_d)) * 0.6 / np.sqrt(in_d) / s[None, :]
        return pack_weight(np.ascontiguousarray(w.T), FMT)

    def lin_b():
        return bf(np.random.standard_normal(H_DIM) * 0.5)

    out = {
        "P": bf(np.random.standard_normal((B, P_DIM)) * sp),
        "hidden": bf(np.random.standard_normal((B, H_DIM)) * sh),
        "cell": bf(np.random.standard_normal((B, H_DIM))),
        "ext_input": bf(np.random.standard_normal((B, X_DIM)) * sx),
    }
    for k in "ifgo":
        out["W_p" + k + "_words"], out["W_p" + k + "_scales"] = lin_w(P_DIM, sp)
        out["b_p" + k] = lin_b()
    for k in "ifgo":
        out["W_h" + k + "_words"], out["W_h" + k + "_scales"] = lin_w(H_DIM, sh)
    for k in "ifgo":
        out["W_x" + k + "_words"], out["W_x" + k + "_scales"] = lin_w(X_DIM, sx)
    return out


def reference(P, hidden, cell, ext_input,
              W_pi_words, W_pi_scales, b_pi, W_pf_words, W_pf_scales, b_pf,
              W_pg_words, W_pg_scales, b_pg, W_po_words, W_po_scales, b_po,
              W_hi_words, W_hi_scales, W_hf_words, W_hf_scales,
              W_hg_words, W_hg_scales, W_ho_words, W_ho_scales,
              W_xi_words, W_xi_scales, W_xf_words, W_xf_scales,
              W_xg_words, W_xg_scales, W_xo_words, W_xo_scales):
    Wp = np.concatenate([unpack_weight(W_pi_words, W_pi_scales, FMT).T, unpack_weight(W_pf_words, W_pf_scales, FMT).T,
                         unpack_weight(W_pg_words, W_pg_scales, FMT).T, unpack_weight(W_po_words, W_po_scales, FMT).T], axis=0)
    bp = np.concatenate([f64(b_pi), f64(b_pf), f64(b_pg), f64(b_po)], axis=0)
    Wh = np.concatenate([unpack_weight(W_hi_words, W_hi_scales, FMT).T, unpack_weight(W_hf_words, W_hf_scales, FMT).T,
                         unpack_weight(W_hg_words, W_hg_scales, FMT).T, unpack_weight(W_ho_words, W_ho_scales, FMT).T], axis=0)
    Wx = np.concatenate([unpack_weight(W_xi_words, W_xi_scales, FMT).T, unpack_weight(W_xf_words, W_xf_scales, FMT).T,
                         unpack_weight(W_xg_words, W_xg_scales, FMT).T, unpack_weight(W_xo_words, W_xo_scales, FMT).T], axis=0)
    gates = ((mxq(f64(P), 1, "e4m3") @ Wp.T) + bp
             + (mxq(f64(hidden), 1, "e4m3") @ Wh.T)
             + (mxq(f64(ext_input), 1, "e4m3") @ Wx.T))
    gi, gf, gg, go = np.split(gates, 4, axis=-1)
    i = sigmoid(gi)
    f = sigmoid(gf)
    g = np.tanh(gg)
    o = sigmoid(go)
    c_new = f * f64(cell) + i * g
    h_new = o * np.tanh(c_new)
    return (h_new, c_new)

@@ -1,0 +1,208 @@
+from contextlib import ExitStack
+
+import concourse.mybir as mybir
+from concourse.masks import make_identity
+
+F32 = mybir.dt.float32
+BF16 = mybir.dt.bfloat16
+U8 = mybir.dt.uint8
+U32 = mybir.dt.uint32
+I32 = mybir.dt.int32
+FP8X4 = mybir.dt.float8_e4m3fn_x4
+ACT = mybir.ActivationFunctionType
+ALU = mybir.AluOpType
+
+B = 128
+H = 1024
+HALF = 512
+K_ALL = 5120
+FLOPS = 2 * B * K_ALL * 4 * H
+
+FIRST_GROUP = {"p": 0, "h": 4, "x": 6}
+N_GROUPS = {"p": 4, "h": 2, "x": 4}
+GATE_ORDER = "igfo"
+GATE_COL = {"i": 0, "f": 1, "g": 2, "o": 3}
+LOOKAHEAD = 8
+
+
+def tile_structuredlstmcell_w_kernel(
+    tc, P, hidden, cell, ext_input,
+    W_pi_words, W_pi_scales, b_pi, W_pf_words, W_pf_scales, b_pf,
+    W_pg_words, W_pg_scales, b_pg, W_po_words, W_po_scales, b_po,
+    W_hi_words, W_hi_scales, W_hf_words, W_hf_scales,
+    W_hg_words, W_hg_scales, W_ho_words, W_ho_scales,
+    W_xi_words, W_xi_scales, W_xf_words, W_xf_scales,
+    W_xg_words, W_xg_scales, W_xo_words, W_xo_scales,
+    out_0, out_1,
+):
+    nc = tc.nc
+    weights = {
+        ("p", "i"): (W_pi_words, W_pi_scales), ("p", "f"): (W_pf_words, W_pf_scales),
+        ("p", "g"): (W_pg_words, W_pg_scales), ("p", "o"): (W_po_words, W_po_scales),
+        ("h", "i"): (W_hi_words, W_hi_scales), ("h", "f"): (W_hf_words, W_hf_scales),
+        ("h", "g"): (W_hg_words, W_hg_scales), ("h", "o"): (W_ho_words, W_ho_scales),
+        ("x", "i"): (W_xi_words, W_xi_scales), ("x", "f"): (W_xf_words, W_xf_scales),
+        ("x", "g"): (W_xg_words, W_xg_scales), ("x", "o"): (W_xo_words, W_xo_scales),
+    }
+    biases = {"i": b_pi, "f": b_pf, "g": b_pg, "o": b_po}
+    stream = [(src, gate) for gate in GATE_ORDER for src in "phx"]
+    n_entries = len(stream)
+
+    with ExitStack() as ctx:
+        ctx.enter_context(tc.manual_schedule())
+        keep = ctx.enter_context(tc.tile_pool(name="keep", bufs=1))
+        wpool = ctx.enter_context(tc.tile_pool(name="wpool", bufs=1))
+        work = ctx.enter_context(tc.tile_pool(name="work", bufs=1))
+        prep = ctx.enter_context(tc.psum_pool(name="prep", bufs=4))
+        accs = ctx.enter_context(tc.psum_pool(name="accs", bufs=4))
+
+        planes = keep.tile([128, n_entries, H], U8, align_bytes=64)
+        brow = keep.tile([128, 4 * H], BF16)
+        ones = keep.tile([128, 128], BF16)
+        ident = keep.tile([128, 128], F32)
+        warm = keep.tile([128, 2], F32)
+        nc.vector.memset(planes[:, 0:3, :].bitcast(I32), 0)
+        nc.vector.memset(warm[:], 0.0)
+        nc.vector.memset(brow[:].bitcast(I32), 0)
+        nc.vector.memset(ones[:], 1.0)
+        nc.vector.memset(planes[:, 3:n_entries, :].bitcast(I32), 0)
+        make_identity(nc, ident[:])
+        nc.scalar.activation(out=warm[:, 1:2], in_=warm[:, 0:1], func=ACT.Sigmoid)
+
+        xs = keep.tile([128, K_ALL], BF16)
+        cell_sb = keep.tile([128, H], BF16)
+        nc.sync.dma_start(out=xs[:, 0:2048], in_=P)
+        nc.sync.dma_start(out=xs[:, 2048:3072], in_=hidden)
+        nc.sync.dma_start(out=xs[:, 3072:5120], in_=ext_input)
+        for gate in "ifgo":
+            col = GATE_COL[gate] * H
+            nc.scalar.dma_start(out=brow[0:1, col:col + H], in_=biases[gate].rearrange("(o n) -> o n", o=1))
+
+        wtiles = {}
+
+        def load_weight(e):
+            src, gate = stream[e]
+            words, scales = weights[(src, gate)]
+            ng = N_GROUPS[src]
+            if ng == 4:
+                wt = wpool.tile([128, 4, 4 * H], U8, name="wbig%d" % e, tag="wbig", bufs=6, align_bytes=64)
+            else:
+                wt = wpool.tile([128, 2, 4 * H], U8, name="wsml%d" % e, tag="wsml", bufs=4, align_bytes=64)
+            wtiles[e] = wt
+            for q in range(4):
+                nc.sync.dma_start(
+                    out=planes[32 * q:32 * q + 4 * ng, e, :].bitcast(I32),
+                    in_=scales[:, 4 * q:4 * q + 4, :].bitcast(I32),
+                )
+            view = words.rearrange("g p n t -> p g (n t)").bitcast(I32)
+            if e < n_entries - 1:
+                nc.sync.dma_start(out=wt[:].bitcast(I32), in_=view)
+            else:
+                nc.sync.dma_start(out=wt[:, 0:2, :].bitcast(I32), in_=view[:, 0:2, :])
+                nc.sync.dma_start(out=wt[:, 2, :].bitcast(I32), in_=view[:, 2, :])
+                nc.sync.dma_start(out=wt[:, 3, 0:2048].bitcast(I32), in_=view[:, 3, 0:HALF])
+                nc.sync.dma_start(out=wt[:, 3, 2048:4096].bitcast(I32), in_=view[:, 3, HALF:H])
+
+        for e in range(LOOKAHEAD):
+            if e == 6:
+                nc.sync.dma_start(out=cell_sb[:], in_=cell)
+            load_weight(e)
+
+        grouped = keep.tile([128, 10, 128, 4], BF16, align_bytes=64)
+        xcodes = keep.tile([128, 10 * 128], U32, align_bytes=64)
+        xscales = keep.tile([128, 10 * 128], U8, align_bytes=64)
+        xs_words = xs[:].bitcast(F32)
+        grouped_words = grouped[:].bitcast(F32)
+
+        banks = []
+        for j in range(5):
+            xt = prep.tile([128, 2, 2, 128], F32, name="xt%d" % j, tag="prep")
+            banks.append(xt)
+            for gg in range(2):
+                g = 2 * j + gg
+                for u in range(2):
+                    nc.tensor.transpose(xt[:, gg, u, :], xs_words[:, 256 * g + u:256 * (g + 1):2], ident[:])
+
+        def copy_bank(j, eng):
+            dst = grouped_words[:, 2 * j:2 * j + 2, :, :]
+            srcv = banks[j][:].rearrange("p g u b -> p g b u")
+            if eng == "v":
+                nc.vector.tensor_copy(out=dst, in_=srcv)
+            else:
+                nc.scalar.copy(out=dst, in_=srcv)
+
+        def quantise(g0, g1):
+            nc.vector.quantize_mx(
+                out=xcodes[:, 128 * g0:128 * g1].bitcast(FP8X4),
+                scales=xscales[:, 128 * g0:128 * g1],
+                in_=grouped[:, g0:g1, :, :].rearrange("p g b t -> p (g b t)"),
+            )
+
+        copy_bank(0, "v")
+        copy_bank(1, "s")
+        copy_bank(2, "v")
+        copy_bank(3, "s")
+        quantise(0, 4)
+        copy_bank(4, "v")
+        quantise(4, 6)
+        quantise(6, 10)
+
+        bias_sb = keep.tile([128, 4 * H], BF16)
+        for j in range(8):
+            pb = prep.tile([128, HALF], F32, name="pb%d" % j, tag="prep")
+            nc.tensor.matmul(out=pb[:], lhsT=ones[:], rhs=brow[:, HALF * j:HALF * (j + 1)], start=True, stop=True)
+            if j % 2 == 0:
+                nc.scalar.copy(out=bias_sb[:, HALF * j:HALF * (j + 1)], in_=pb[:])
+            else:
+                nc.vector.tensor_copy(out=bias_sb[:, HALF * j:HALF * (j + 1)], in_=pb[:])
+
+        acts = {}
+        for gate in GATE_ORDER:
+            acts[gate] = work.tile([128, H], F32, name="act_" + gate)
+        c_new = work.tile([128, H], F32)
+        tanh_c = work.tile([128, H], F32)
+
+        acc = {}
+        for e in range(n_entries):
+            src, gate = stream[e]
+            if src == "p":
+                for h in range(2):
+                    acc[h] = accs.tile([128, HALF], F32, name="acc_%s%d" % (gate, h), tag="acc")
+            wt = wtiles[e]
+            for g in range(N_GROUPS[src]):
+                gx = FIRST_GROUP[src] + g
+                for h in range(2):
+                    nc.tensor.matmul_mx(
+                        out=acc[h][:],
+                        lhsT=xcodes[:, 128 * gx:128 * (gx + 1)].bitcast(FP8X4),
+                        lhsT_scale=xscales[:, 128 * gx:128 * (gx + 1)],
+                        rhs=wt[:, g, 2048 * h:2048 * (h + 1)].bitcast(FP8X4),
+                        rhs_scale=planes[4 * g:128, e, HALF * h:HALF * (h + 1)],
+                        start=(gx == 0),
+                        stop=(gx == 9),
+                    )
+            if e + LOOKAHEAD < n_entries:
+                load_weight(e + LOOKAHEAD)
+            if src != "x":
+                continue
+            func = ACT.Tanh if gate == "g" else ACT.Sigmoid
+            col = GATE_COL[gate] * H
+            pres = []
+            for h in range(2):
+                pre = work.tile([128, HALF], F32, name="pre_%s%d" % (gate, h), tag="pre", bufs=3)
+                pres.append(pre)
+                nc.vector.tensor_tensor(out=pre[:], in0=acc[h][:], in1=bias_sb[:, col + HALF * h:col + HALF * (h + 1)], op=ALU.add)
+            for h in range(2):
+                nc.scalar.activation(out=acts[gate][:, HALF * h:HALF * (h + 1)], in_=pres[h][:], func=func)
+            if gate == "g":
+                nc.vector.tensor_tensor(out=acts["i"][:], in0=acts["i"][:], in1=acts["g"][:], op=ALU.mult)
+            if gate == "f":
+                nc.vector.tensor_tensor(out=acts["f"][:], in0=acts["f"][:], in1=cell_sb[:], op=ALU.mult)
+                nc.vector.tensor_tensor(out=c_new[:], in0=acts["f"][:], in1=acts["i"][:], op=ALU.add)
+                nc.scalar.activation(out=tanh_c[:], in_=c_new[:], func=ACT.Tanh)
+                nc.sync.dma_start(out=out_1, in_=c_new[:])
+            if gate == "o":
+                for h in range(2):
+                    cols = slice(HALF * h, HALF * (h + 1))
+                    nc.vector.tensor_tensor(out=acts["o"][:, cols], in0=acts["o"][:, cols], in1=tanh_c[:, cols], op=ALU.mult)
+                    nc.sync.dma_start(out=out_0[:, cols], in_=acts["o"][:, cols])

@@ -61,12 +61,19 @@ def tile_structuredlstmcell_w_kernel(
         ones = keep.tile([128, 128], BF16)
         ident = keep.tile([128, 128], F32)
         warm = keep.tile([128, 2], F32)
-        nc.vector.memset(planes[:, 0:3, :].bitcast(I32), 0)
+        nc.vector.memset(planes[:].bitcast(I32), 0)
         nc.vector.memset(warm[:], 0.0)
         nc.vector.memset(brow[:].bitcast(I32), 0)
         nc.vector.memset(ones[:], 1.0)
-        nc.vector.memset(planes[:, 3:n_entries, :].bitcast(I32), 0)
         make_identity(nc, ident[:])
+        for e in range(n_entries):
+            scales = weights[stream[e]][1]
+            ng = N_GROUPS[stream[e][0]]
+            for q in range(4):
+                nc.gpsimd.dma_start(
+                    out=planes[32 * q:32 * q + 4 * ng, e, :].bitcast(F32),
+                    in_=scales[:, 4 * q:4 * q + 4, :].bitcast(F32),
+                )
         nc.scalar.activation(out=warm[:, 1:2], in_=warm[:, 0:1], func=ACT.Sigmoid)
 
         xs = keep.tile([128, K_ALL], BF16)
@@ -89,11 +96,6 @@ def tile_structuredlstmcell_w_kernel(
             else:
                 wt = wpool.tile([128, 2, 4 * H], U8, name="wsml%d" % e, tag="wsml", bufs=4, align_bytes=64)
             wtiles[e] = wt
-            for q in range(4):
-                nc.sync.dma_start(
-                    out=planes[32 * q:32 * q + 4 * ng, e, :].bitcast(I32),
-                    in_=scales[:, 4 * q:4 * q + 4, :].bitcast(I32),
-                )
             view = words.rearrange("g p n t -> p g (n t)").bitcast(I32)
             if e < n_entries - 1:
                 nc.sync.dma_start(out=wt[:].bitcast(I32), in_=view)

@@ -97,13 +97,12 @@ def tile_structuredlstmcell_w_kernel(
                 wt = wpool.tile([128, 2, 4 * H], U8, name="wsml%d" % e, tag="wsml", bufs=4, align_bytes=64)
             wtiles[e] = wt
             view = words.rearrange("g p n t -> p g (n t)").bitcast(I32)
-            if e < n_entries - 1:
-                nc.sync.dma_start(out=wt[:].bitcast(I32), in_=view)
-            else:
-                nc.sync.dma_start(out=wt[:, 0:2, :].bitcast(I32), in_=view[:, 0:2, :])
-                nc.sync.dma_start(out=wt[:, 2, :].bitcast(I32), in_=view[:, 2, :])
-                nc.sync.dma_start(out=wt[:, 3, 0:2048].bitcast(I32), in_=view[:, 3, 0:HALF])
-                nc.sync.dma_start(out=wt[:, 3, 2048:4096].bitcast(I32), in_=view[:, 3, HALF:H])
+            for g in range(ng):
+                if e < n_entries - 1 or g < ng - 1:
+                    nc.sync.dma_start(out=wt[:, g, :].bitcast(I32), in_=view[:, g, :])
+                else:
+                    nc.sync.dma_start(out=wt[:, g, 0:2048].bitcast(I32), in_=view[:, g, 0:HALF])
+                    nc.sync.dma_start(out=wt[:, g, 2048:4096].bitcast(I32), in_=view[:, g, HALF:H])
 
         for e in range(LOOKAHEAD):
             if e == 6:

@@ -23,6 +23,7 @@ N_GROUPS = {"p": 4, "h": 2, "x": 4}
 GATE_ORDER = "igfo"
 GATE_COL = {"i": 0, "f": 1, "g": 2, "o": 3}
 LOOKAHEAD = 8
+HW_SCALES = 2
 
 
 def tile_structuredlstmcell_w_kernel(
@@ -61,19 +62,25 @@ def tile_structuredlstmcell_w_kernel(
         ones = keep.tile([128, 128], BF16)
         ident = keep.tile([128, 128], F32)
         warm = keep.tile([128, 2], F32)
-        nc.vector.memset(planes[:].bitcast(I32), 0)
+        nc.vector.memset(planes[:, 0:HW_SCALES, :].bitcast(I32), 0)
+        nc.vector.memset(planes[:, HW_SCALES:n_entries, :].bitcast(I32), 0)
         nc.vector.memset(warm[:], 0.0)
-        nc.vector.memset(brow[:].bitcast(I32), 0)
         nc.vector.memset(ones[:], 1.0)
         make_identity(nc, ident[:])
-        for e in range(n_entries):
+
+        def load_scales(e):
             scales = weights[stream[e]][1]
             ng = N_GROUPS[stream[e][0]]
             for q in range(4):
-                nc.gpsimd.dma_start(
-                    out=planes[32 * q:32 * q + 4 * ng, e, :].bitcast(F32),
-                    in_=scales[:, 4 * q:4 * q + 4, :].bitcast(F32),
-                )
+                dst = planes[32 * q:32 * q + 4 * ng, e, :]
+                srcv = scales[:, 4 * q:4 * q + 4, :]
+                if e < HW_SCALES:
+                    nc.sync.dma_start(out=dst.bitcast(I32), in_=srcv.bitcast(I32))
+                else:
+                    nc.gpsimd.dma_start(out=dst.bitcast(F32), in_=srcv.bitcast(F32))
+
+        for e in range(HW_SCALES, n_entries):
+            load_scales(e)
         nc.scalar.activation(out=warm[:, 1:2], in_=warm[:, 0:1], func=ACT.Sigmoid)
 
         xs = keep.tile([128, K_ALL], BF16)
@@ -81,9 +88,8 @@ def tile_structuredlstmcell_w_kernel(
         nc.sync.dma_start(out=xs[:, 0:2048], in_=P)
         nc.sync.dma_start(out=xs[:, 2048:3072], in_=hidden)
         nc.sync.dma_start(out=xs[:, 3072:5120], in_=ext_input)
-        for gate in "ifgo":
-            col = GATE_COL[gate] * H
-            nc.scalar.dma_start(out=brow[0:1, col:col + H], in_=biases[gate].rearrange("(o n) -> o n", o=1))
+        for e in range(HW_SCALES):
+            load_scales(e)
 
         wtiles = {}
 
@@ -149,13 +155,19 @@ def tile_structuredlstmcell_w_kernel(
         quantise(6, 10)
 
         bias_sb = keep.tile([128, 4 * H], BF16)
-        for j in range(8):
-            pb = prep.tile([128, HALF], F32, name="pb%d" % j, tag="prep")
-            nc.tensor.matmul(out=pb[:], lhsT=ones[:], rhs=brow[:, HALF * j:HALF * (j + 1)], start=True, stop=True)
-            if j % 2 == 0:
-                nc.scalar.copy(out=bias_sb[:, HALF * j:HALF * (j + 1)], in_=pb[:])
-            else:
-                nc.vector.tensor_copy(out=bias_sb[:, HALF * j:HALF * (j + 1)], in_=pb[:])
+        nc.vector.memset(brow[:].bitcast(I32), 0)
+        for gate in "ifgo":
+            col = GATE_COL[gate] * H
+            nc.scalar.dma_start(out=brow[0:1, col:col + H], in_=biases[gate].rearrange("(o n) -> o n", o=1))
+
+        def spread_biases():
+            for j in range(8):
+                pb = prep.tile([128, HALF], F32, name="pb%d" % j, tag="prep")
+                nc.tensor.matmul(out=pb[:], lhsT=ones[:], rhs=brow[:, HALF * j:HALF * (j + 1)], start=True, stop=True)
+                if j % 2 == 0:
+                    nc.scalar.copy(out=bias_sb[:, HALF * j:HALF * (j + 1)], in_=pb[:])
+                else:
+                    nc.vector.tensor_copy(out=bias_sb[:, HALF * j:HALF * (j + 1)], in_=pb[:])
 
         acts = {}
         for gate in GATE_ORDER:
@@ -184,6 +196,8 @@ def tile_structuredlstmcell_w_kernel(
                     )
             if e + LOOKAHEAD < n_entries:
                 load_weight(e + LOOKAHEAD)
+            if e == 1:
+                spread_biases()
             if src != "x":
                 continue
             func = ACT.Tanh if gate == "g" else ACT.Sigmoid

@@ -23,7 +23,13 @@ N_GROUPS = {"p": 4, "h": 2, "x": 4}
 GATE_ORDER = "igfo"
 GATE_COL = {"i": 0, "f": 1, "g": 2, "o": 3}
 LOOKAHEAD = 8
-HW_SCALES = 2
+H_PLANE_OFFSET = {"i": 0, "g": 8, "f": 0, "o": 8}
+PIECES = {
+    "i": [(0, 512), (512, 512)],
+    "g": [(0, 512), (512, 512)],
+    "f": [(0, 512), (512, 512)],
+    "o": [(0, 512), (512, 256), (768, 256)],
+}
 
 
 def tile_structuredlstmcell_w_kernel(
@@ -54,33 +60,30 @@ def tile_structuredlstmcell_w_kernel(
         keep = ctx.enter_context(tc.tile_pool(name="keep", bufs=1))
         wpool = ctx.enter_context(tc.tile_pool(name="wpool", bufs=1))
         work = ctx.enter_context(tc.tile_pool(name="work", bufs=1))
-        prep = ctx.enter_context(tc.psum_pool(name="prep", bufs=4))
-        accs = ctx.enter_context(tc.psum_pool(name="accs", bufs=4))
+        prep = ctx.enter_context(tc.psum_pool(name="prep", bufs=3))
+        accs = ctx.enter_context(tc.psum_pool(name="accs", bufs=5))
 
         planes = keep.tile([128, n_entries, H], U8, align_bytes=64)
         brow = keep.tile([128, 4 * H], BF16)
         ones = keep.tile([128, 128], BF16)
         ident = keep.tile([128, 128], F32)
         warm = keep.tile([128, 2], F32)
-        nc.vector.memset(planes[:, 0:HW_SCALES, :].bitcast(I32), 0)
-        nc.vector.memset(planes[:, HW_SCALES:n_entries, :].bitcast(I32), 0)
+        nc.vector.memset(planes[:].bitcast(I32), 0)
         nc.vector.memset(warm[:], 0.0)
+        nc.vector.memset(brow[:].bitcast(I32), 0)
         nc.vector.memset(ones[:], 1.0)
         make_identity(nc, ident[:])
-
-        def load_scales(e):
+        plane_offset = []
+        for e in range(n_entries):
             scales = weights[stream[e]][1]
             ng = N_GROUPS[stream[e][0]]
+            off = H_PLANE_OFFSET[stream[e][1]] if ng == 2 else 0
+            plane_offset.append(off)
             for q in range(4):
-                dst = planes[32 * q:32 * q + 4 * ng, e, :]
-                srcv = scales[:, 4 * q:4 * q + 4, :]
-                if e < HW_SCALES:
-                    nc.sync.dma_start(out=dst.bitcast(I32), in_=srcv.bitcast(I32))
-                else:
-                    nc.gpsimd.dma_start(out=dst.bitcast(F32), in_=srcv.bitcast(F32))
-
-        for e in range(HW_SCALES, n_entries):
-            load_scales(e)
+                nc.gpsimd.dma_start(
+                    out=planes[32 * q + off:32 * q + off + 4 * ng, e, :].bitcast(F32),
+                    in_=scales[:, 4 * q:4 * q + 4, :].bitcast(F32),
+                )
         nc.scalar.activation(out=warm[:, 1:2], in_=warm[:, 0:1], func=ACT.Sigmoid)
 
         xs = keep.tile([128, K_ALL], BF16)
@@ -88,8 +91,9 @@ def tile_structuredlstmcell_w_kernel(
         nc.sync.dma_start(out=xs[:, 0:2048], in_=P)
         nc.sync.dma_start(out=xs[:, 2048:3072], in_=hidden)
         nc.sync.dma_start(out=xs[:, 3072:5120], in_=ext_input)
-        for e in range(HW_SCALES):
-            load_scales(e)
+        for gate in "ifgo":
+            col = GATE_COL[gate] * H
+            nc.scalar.dma_start(out=brow[0:1, col:col + H], in_=biases[gate].rearrange("(o n) -> o n", o=1))
 
         wtiles = {}
 
@@ -103,12 +107,15 @@ def tile_structuredlstmcell_w_kernel(
                 wt = wpool.tile([128, 2, 4 * H], U8, name="wsml%d" % e, tag="wsml", bufs=4, align_bytes=64)
             wtiles[e] = wt
             view = words.rearrange("g p n t -> p g (n t)").bitcast(I32)
-            for g in range(ng):
-                if e < n_entries - 1 or g < ng - 1:
+            if e < n_entries - 1:
+                for g in range(ng):
                     nc.sync.dma_start(out=wt[:, g, :].bitcast(I32), in_=view[:, g, :])
-                else:
-                    nc.sync.dma_start(out=wt[:, g, 0:2048].bitcast(I32), in_=view[:, g, 0:HALF])
-                    nc.sync.dma_start(out=wt[:, g, 2048:4096].bitcast(I32), in_=view[:, g, HALF:H])
+            else:
+                for g in range(ng):
+                    nc.sync.dma_start(out=wt[:, g, 0:2048].bitcast(I32), in_=view[:, g, 0:512])
+                nc.sync.dma_start(out=wt[:, 0:2, 2048:4096].bitcast(I32), in_=view[:, 0:2, 512:1024])
+                nc.sync.dma_start(out=wt[:, 2:4, 2048:3072].bitcast(I32), in_=view[:, 2:4, 512:768])
+                nc.sync.dma_start(out=wt[:, 2:4, 3072:4096].bitcast(I32), in_=view[:, 2:4, 768:1024])
 
         for e in range(LOOKAHEAD):
             if e == 6:
@@ -155,19 +162,13 @@ def tile_structuredlstmcell_w_kernel(
         quantise(6, 10)
 
         bias_sb = keep.tile([128, 4 * H], BF16)
-        nc.vector.memset(brow[:].bitcast(I32), 0)
-        for gate in "ifgo":
-            col = GATE_COL[gate] * H
-            nc.scalar.dma_start(out=brow[0:1, col:col + H], in_=biases[gate].rearrange("(o n) -> o n", o=1))
-
-        def spread_biases():
-            for j in range(8):
-                pb = prep.tile([128, HALF], F32, name="pb%d" % j, tag="prep")
-                nc.tensor.matmul(out=pb[:], lhsT=ones[:], rhs=brow[:, HALF * j:HALF * (j + 1)], start=True, stop=True)
-                if j % 2 == 0:
-                    nc.scalar.copy(out=bias_sb[:, HALF * j:HALF * (j + 1)], in_=pb[:])
-                else:
-                    nc.vector.tensor_copy(out=bias_sb[:, HALF * j:HALF * (j + 1)], in_=pb[:])
+        for j in range(8):
+            pb = prep.tile([128, HALF], F32, name="pb%d" % j, tag="prep")
+            nc.tensor.matmul(out=pb[:], lhsT=ones[:], rhs=brow[:, HALF * j:HALF * (j + 1)], start=True, stop=True)
+            if j % 2 == 0:
+                nc.scalar.copy(out=bias_sb[:, HALF * j:HALF * (j + 1)], in_=pb[:])
+            else:
+                nc.vector.tensor_copy(out=bias_sb[:, HALF * j:HALF * (j + 1)], in_=pb[:])
 
         acts = {}
         for gate in GATE_ORDER:
@@ -176,39 +177,60 @@ def tile_structuredlstmcell_w_kernel(
         tanh_c = work.tile([128, H], F32)
 
         acc = {}
+
+        def one_pass(e, g, k):
+            src, gate = stream[e]
+            c0, w = PIECES[gate][k]
+            gx = FIRST_GROUP[src] + g
+            nc.tensor.matmul_mx(
+                out=acc[k][:],
+                lhsT=xcodes[:, 128 * gx:128 * (gx + 1)].bitcast(FP8X4),
+                lhsT_scale=xscales[:, 128 * gx:128 * (gx + 1)],
+                rhs=wtiles[e][:, g, 4 * c0:4 * (c0 + w)].bitcast(FP8X4),
+                rhs_scale=planes[plane_offset[e] + 4 * g:128, e, c0:c0 + w],
+                start=(gx == 0),
+                stop=(gx == 9),
+            )
+
+        pres = {}
+
+        def add_bias(gate, k):
+            c0, w = PIECES[gate][k]
+            col = GATE_COL[gate] * H + c0
+            pre = work.tile([128, w], F32, name="pre_%s%d" % (gate, k), tag="pre", bufs=3)
+            pres[k] = pre
+            nc.vector.tensor_tensor(out=pre[:], in0=acc[k][:], in1=bias_sb[:, col:col + w], op=ALU.add)
+
+        def squash(gate, k):
+            c0, w = PIECES[gate][k]
+            func = ACT.Tanh if gate == "g" else ACT.Sigmoid
+            nc.scalar.activation(out=acts[gate][:, c0:c0 + w], in_=pres[k][:], func=func)
+
+        def finish_h(k):
+            c0, w = PIECES["o"][k]
+            cols = slice(c0, c0 + w)
+            nc.vector.tensor_tensor(out=acts["o"][:, cols], in0=acts["o"][:, cols], in1=tanh_c[:, cols], op=ALU.mult)
+            nc.sync.dma_start(out=out_0[:, cols], in_=acts["o"][:, cols])
+
         for e in range(n_entries):
             src, gate = stream[e]
+            n_pieces = len(PIECES[gate])
             if src == "p":
-                for h in range(2):
-                    acc[h] = accs.tile([128, HALF], F32, name="acc_%s%d" % (gate, h), tag="acc")
-            wt = wtiles[e]
-            for g in range(N_GROUPS[src]):
-                gx = FIRST_GROUP[src] + g
-                for h in range(2):
-                    nc.tensor.matmul_mx(
-                        out=acc[h][:],
-                        lhsT=xcodes[:, 128 * gx:128 * (gx + 1)].bitcast(FP8X4),
-                        lhsT_scale=xscales[:, 128 * gx:128 * (gx + 1)],
-                        rhs=wt[:, g, 2048 * h:2048 * (h + 1)].bitcast(FP8X4),
-                        rhs_scale=planes[4 * g:128, e, HALF * h:HALF * (h + 1)],
-                        start=(gx == 0),
-                        stop=(gx == 9),
-                    )
+                for k in range(n_pieces):
+                    acc[k] = accs.tile([128, PIECES[gate][k][1]], F32, name="acc_%s%d" % (gate, k), tag="acc")
+            if e < n_entries - 1:
+                for g in range(N_GROUPS[src]):
+                    for k in range(n_pieces):
+                        one_pass(e, g, k)
             if e + LOOKAHEAD < n_entries:
                 load_weight(e + LOOKAHEAD)
-            if e == 1:
-                spread_biases()
             if src != "x":
                 continue
-            func = ACT.Tanh if gate == "g" else ACT.Sigmoid
-            col = GATE_COL[gate] * H
-            pres = []
-            for h in range(2):
-                pre = work.tile([128, HALF], F32, name="pre_%s%d" % (gate, h), tag="pre", bufs=3)
-                pres.append(pre)
-                nc.vector.tensor_tensor(out=pre[:], in0=acc[h][:], in1=bias_sb[:, col + HALF * h:col + HALF * (h + 1)], op=ALU.add)
-            for h in range(2):
-                nc.scalar.activation(out=acts[gate][:, HALF * h:HALF * (h + 1)], in_=pres[h][:], func=func)
+            if gate != "o":
+                for k in range(n_pieces):
+                    add_bias(gate, k)
+                for k in range(n_pieces):
+                    squash(gate, k)
             if gate == "g":
                 nc.vector.tensor_tensor(out=acts["i"][:], in0=acts["i"][:], in1=acts["g"][:], op=ALU.mult)
             if gate == "f":
@@ -217,7 +239,20 @@ def tile_structuredlstmcell_w_kernel(
                 nc.scalar.activation(out=tanh_c[:], in_=c_new[:], func=ACT.Tanh)
                 nc.sync.dma_start(out=out_1, in_=c_new[:])
             if gate == "o":
-                for h in range(2):
-                    cols = slice(HALF * h, HALF * (h + 1))
-                    nc.vector.tensor_tensor(out=acts["o"][:, cols], in0=acts["o"][:, cols], in1=tanh_c[:, cols], op=ALU.mult)
-                    nc.sync.dma_start(out=out_0[:, cols], in_=acts["o"][:, cols])
+                for g in range(4):
+                    one_pass(e, g, 0)
+                add_bias(gate, 0)
+                squash(gate, 0)
+                finish_h(0)
+                for g in range(2):
+                    one_pass(e, g, 1)
+                    one_pass(e, g, 2)
+                for k in (1, 2):
+                    one_pass(e, 2, k)
+                    one_pass(e, 3, k)
+                add_bias(gate, 1)
+                add_bias(gate, 2)
+                squash(gate, 1)
+                squash(gate, 2)
+                finish_h(1)
+                finish_h(2)

@@ -21,8 +21,8 @@ FLOPS = 2 * B * K_ALL * 4 * H
 FIRST_GROUP = {"p": 0, "h": 4, "x": 6}
 N_GROUPS = {"p": 4, "h": 2, "x": 4}
 GATE_ORDER = "igfo"
-GATE_COL = {"i": 0, "f": 1, "g": 2, "o": 3}
-LOOKAHEAD = 8
+GATE_ROW = {"i": 0, "f": 1, "g": 2, "o": 3}
+LOOKAHEAD = 4
 H_PLANE_OFFSET = {"i": 0, "g": 8, "f": 0, "o": 8}
 PIECES = {
     "i": [(0, 512), (512, 512)],
@@ -59,19 +59,18 @@ def tile_structuredlstmcell_w_kernel(
         ctx.enter_context(tc.manual_schedule())
         keep = ctx.enter_context(tc.tile_pool(name="keep", bufs=1))
         wpool = ctx.enter_context(tc.tile_pool(name="wpool", bufs=1))
-        work = ctx.enter_context(tc.tile_pool(name="work", bufs=1))
         prep = ctx.enter_context(tc.psum_pool(name="prep", bufs=3))
         accs = ctx.enter_context(tc.psum_pool(name="accs", bufs=5))
 
         planes = keep.tile([128, n_entries, H], U8, align_bytes=64)
-        brow = keep.tile([128, 4 * H], BF16)
-        ones = keep.tile([128, 128], BF16)
+        brow = keep.tile([128, H], BF16)
         ident = keep.tile([128, 128], F32)
+        ident_bf = keep.tile([128, 128], BF16)
         warm = keep.tile([128, 2], F32)
-        nc.vector.memset(planes[:].bitcast(I32), 0)
+        nc.vector.memset(planes[:, 0:3, :].bitcast(I32), 0)
         nc.vector.memset(warm[:], 0.0)
         nc.vector.memset(brow[:].bitcast(I32), 0)
-        nc.vector.memset(ones[:], 1.0)
+        nc.vector.memset(planes[:, 3:n_entries, :].bitcast(I32), 0)
         make_identity(nc, ident[:])
         plane_offset = []
         for e in range(n_entries):
@@ -91,9 +90,6 @@ def tile_structuredlstmcell_w_kernel(
         nc.sync.dma_start(out=xs[:, 0:2048], in_=P)
         nc.sync.dma_start(out=xs[:, 2048:3072], in_=hidden)
         nc.sync.dma_start(out=xs[:, 3072:5120], in_=ext_input)
-        for gate in "ifgo":
-            col = GATE_COL[gate] * H
-            nc.scalar.dma_start(out=brow[0:1, col:col + H], in_=biases[gate].rearrange("(o n) -> o n", o=1))
 
         wtiles = {}
 
@@ -101,26 +97,28 @@ def tile_structuredlstmcell_w_kernel(
             src, gate = stream[e]
             words, scales = weights[(src, gate)]
             ng = N_GROUPS[src]
-            if ng == 4:
-                wt = wpool.tile([128, 4, 4 * H], U8, name="wbig%d" % e, tag="wbig", bufs=6, align_bytes=64)
-            else:
-                wt = wpool.tile([128, 2, 4 * H], U8, name="wsml%d" % e, tag="wsml", bufs=4, align_bytes=64)
+            wt = wpool.tile([128, ng, 4 * H], U8, name="w%d" % e, align_bytes=64)
             wtiles[e] = wt
             view = words.rearrange("g p n t -> p g (n t)").bitcast(I32)
             if e < n_entries - 1:
                 for g in range(ng):
-                    nc.sync.dma_start(out=wt[:, g, :].bitcast(I32), in_=view[:, g, :])
+                    queue = nc.sync if g % 2 == 0 else nc.scalar
+                    queue.dma_start(out=wt[:, g, :].bitcast(I32), in_=view[:, g, :])
             else:
                 for g in range(ng):
-                    nc.sync.dma_start(out=wt[:, g, 0:2048].bitcast(I32), in_=view[:, g, 0:512])
+                    queue = nc.sync if g % 2 == 0 else nc.scalar
+                    queue.dma_start(out=wt[:, g, 0:2048].bitcast(I32), in_=view[:, g, 0:512])
                 nc.sync.dma_start(out=wt[:, 0:2, 2048:4096].bitcast(I32), in_=view[:, 0:2, 512:1024])
-                nc.sync.dma_start(out=wt[:, 2:4, 2048:3072].bitcast(I32), in_=view[:, 2:4, 512:768])
+                nc.scalar.dma_start(out=wt[:, 2:4, 2048:3072].bitcast(I32), in_=view[:, 2:4, 512:768])
                 nc.sync.dma_start(out=wt[:, 2:4, 3072:4096].bitcast(I32), in_=view[:, 2:4, 768:1024])
 
         for e in range(LOOKAHEAD):
-            if e == 6:
-                nc.sync.dma_start(out=cell_sb[:], in_=cell)
+            if e == 1:
+                for gate in "ifgo":
+                    row = 32 * GATE_ROW[gate]
+                    nc.scalar.dma_start(out=brow[row:row + 1, :], in_=biases[gate].rearrange("(o n) -> o n", o=1))
             load_weight(e)
+        nc.sync.dma_start(out=cell_sb[:], in_=cell)
 
         grouped = keep.tile([128, 10, 128, 4], BF16, align_bytes=64)
         xcodes = keep.tile([128, 10 * 128], U32, align_bytes=64)
@@ -128,22 +126,16 @@ def tile_structuredlstmcell_w_kernel(
         xs_words = xs[:].bitcast(F32)
         grouped_words = grouped[:].bitcast(F32)
 
-        banks = []
-        for j in range(5):
+        def transpose_bank(j):
             xt = prep.tile([128, 2, 2, 128], F32, name="xt%d" % j, tag="prep")
-            banks.append(xt)
             for gg in range(2):
                 g = 2 * j + gg
                 for u in range(2):
                     nc.tensor.transpose(xt[:, gg, u, :], xs_words[:, 256 * g + u:256 * (g + 1):2], ident[:])
-
-        def copy_bank(j, eng):
-            dst = grouped_words[:, 2 * j:2 * j + 2, :, :]
-            srcv = banks[j][:].rearrange("p g u b -> p g b u")
-            if eng == "v":
-                nc.vector.tensor_copy(out=dst, in_=srcv)
-            else:
-                nc.scalar.copy(out=dst, in_=srcv)
+            nc.vector.tensor_copy(
+                out=grouped_words[:, 2 * j:2 * j + 2, :, :],
+                in_=xt[:].rearrange("p g u b -> p g b u"),
+            )
 
         def quantise(g0, g1):
             nc.vector.quantize_mx(
@@ -152,29 +144,34 @@ def tile_structuredlstmcell_w_kernel(
                 in_=grouped[:, g0:g1, :, :].rearrange("p g b t -> p (g b t)"),
             )
 
-        copy_bank(0, "v")
-        copy_bank(1, "s")
-        copy_bank(2, "v")
-        copy_bank(3, "s")
+        for j in range(3):
+            transpose_bank(j)
         quantise(0, 4)
-        copy_bank(4, "v")
+        transpose_bank(3)
         quantise(4, 6)
+        transpose_bank(4)
+        nc.vector.tensor_copy(out=ident_bf[:], in_=ident[:])
         quantise(6, 10)
 
-        bias_sb = keep.tile([128, 4 * H], BF16)
-        for j in range(8):
-            pb = prep.tile([128, HALF], F32, name="pb%d" % j, tag="prep")
-            nc.tensor.matmul(out=pb[:], lhsT=ones[:], rhs=brow[:, HALF * j:HALF * (j + 1)], start=True, stop=True)
-            if j % 2 == 0:
-                nc.scalar.copy(out=bias_sb[:, HALF * j:HALF * (j + 1)], in_=pb[:])
-            else:
-                nc.vector.tensor_copy(out=bias_sb[:, HALF * j:HALF * (j + 1)], in_=pb[:])
+        bias_sb = keep.tile([128, 4, H], BF16)
+
+        def spread_bias(gate):
+            row = GATE_ROW[gate]
+            for h in range(2):
+                pb = prep.tile([128, HALF], F32, name="pb_%s%d" % (gate, h), tag="prep")
+                nc.tensor.matmul(
+                    out=pb[:],
+                    lhsT=ident_bf[:, 32 * row:32 * row + 1].to_broadcast([128, 128]),
+                    rhs=brow[:, HALF * h:HALF * (h + 1)],
+                    start=True, stop=True,
+                )
+                nc.vector.tensor_copy(out=bias_sb[:, row, HALF * h:HALF * (h + 1)], in_=pb[:])
 
         acts = {}
         for gate in GATE_ORDER:
-            acts[gate] = work.tile([128, H], F32, name="act_" + gate)
-        c_new = work.tile([128, H], F32)
-        tanh_c = work.tile([128, H], F32)
+            acts[gate] = keep.tile([128, H], F32, name="act_" + gate)
+        c_new = acts["f"]
+        tanh_c = acts["g"]
 
         acc = {}
 
@@ -192,19 +189,17 @@ def tile_structuredlstmcell_w_kernel(
                 stop=(gx == 9),
             )
 
-        pres = {}
-
         def add_bias(gate, k):
             c0, w = PIECES[gate][k]
-            col = GATE_COL[gate] * H + c0
-            pre = work.tile([128, w], F32, name="pre_%s%d" % (gate, k), tag="pre", bufs=3)
-            pres[k] = pre
-            nc.vector.tensor_tensor(out=pre[:], in0=acc[k][:], in1=bias_sb[:, col:col + w], op=ALU.add)
+            nc.vector.tensor_tensor(
+                out=acts[gate][:, c0:c0 + w], in0=acc[k][:],
+                in1=bias_sb[:, GATE_ROW[gate], c0:c0 + w], op=ALU.add,
+            )
 
         def squash(gate, k):
             c0, w = PIECES[gate][k]
             func = ACT.Tanh if gate == "g" else ACT.Sigmoid
-            nc.scalar.activation(out=acts[gate][:, c0:c0 + w], in_=pres[k][:], func=func)
+            nc.scalar.activation(out=acts[gate][:, c0:c0 + w], in_=acts[gate][:, c0:c0 + w], func=func)
 
         def finish_h(k):
             c0, w = PIECES["o"][k]
@@ -215,15 +210,17 @@ def tile_structuredlstmcell_w_kernel(
         for e in range(n_entries):
             src, gate = stream[e]
             n_pieces = len(PIECES[gate])
+            if e + LOOKAHEAD < n_entries:
+                load_weight(e + LOOKAHEAD)
             if src == "p":
                 for k in range(n_pieces):
                     acc[k] = accs.tile([128, PIECES[gate][k][1]], F32, name="acc_%s%d" % (gate, k), tag="acc")
+            if src == "x":
+                spread_bias(gate)
             if e < n_entries - 1:
                 for g in range(N_GROUPS[src]):
                     for k in range(n_pieces):
                         one_pass(e, g, k)
-            if e + LOOKAHEAD < n_entries:
-                load_weight(e + LOOKAHEAD)
             if src != "x":
                 continue
             if gate != "o":

@@ -22,7 +22,6 @@ FIRST_GROUP = {"p": 0, "h": 4, "x": 6}
 N_GROUPS = {"p": 4, "h": 2, "x": 4}
 GATE_ORDER = "igfo"
 GATE_ROW = {"i": 0, "f": 1, "g": 2, "o": 3}
-LOOKAHEAD = 4
 H_PLANE_OFFSET = {"i": 0, "g": 8, "f": 0, "o": 8}
 PIECES = {
     "i": [(0, 512), (512, 512)],
@@ -102,23 +101,22 @@ def tile_structuredlstmcell_w_kernel(
             view = words.rearrange("g p n t -> p g (n t)").bitcast(I32)
             if e < n_entries - 1:
                 for g in range(ng):
-                    queue = nc.sync if g % 2 == 0 else nc.scalar
-                    queue.dma_start(out=wt[:, g, :].bitcast(I32), in_=view[:, g, :])
+                    nc.sync.dma_start(out=wt[:, g, :].bitcast(I32), in_=view[:, g, :])
             else:
                 for g in range(ng):
-                    queue = nc.sync if g % 2 == 0 else nc.scalar
-                    queue.dma_start(out=wt[:, g, 0:2048].bitcast(I32), in_=view[:, g, 0:512])
+                    nc.sync.dma_start(out=wt[:, g, 0:2048].bitcast(I32), in_=view[:, g, 0:512])
                 nc.sync.dma_start(out=wt[:, 0:2, 2048:4096].bitcast(I32), in_=view[:, 0:2, 512:1024])
-                nc.scalar.dma_start(out=wt[:, 2:4, 2048:3072].bitcast(I32), in_=view[:, 2:4, 512:768])
+                nc.sync.dma_start(out=wt[:, 2:4, 2048:3072].bitcast(I32), in_=view[:, 2:4, 512:768])
                 nc.sync.dma_start(out=wt[:, 2:4, 3072:4096].bitcast(I32), in_=view[:, 2:4, 768:1024])
 
-        for e in range(LOOKAHEAD):
+        for e in range(n_entries):
             if e == 1:
                 for gate in "ifgo":
                     row = 32 * GATE_ROW[gate]
                     nc.scalar.dma_start(out=brow[row:row + 1, :], in_=biases[gate].rearrange("(o n) -> o n", o=1))
+            if e == 6:
+                nc.sync.dma_start(out=cell_sb[:], in_=cell)
             load_weight(e)
-        nc.sync.dma_start(out=cell_sb[:], in_=cell)
 
         grouped = keep.tile([128, 10, 128, 4], BF16, align_bytes=64)
         xcodes = keep.tile([128, 10 * 128], U32, align_bytes=64)
@@ -210,8 +208,6 @@ def tile_structuredlstmcell_w_kernel(
         for e in range(n_entries):
             src, gate = stream[e]
             n_pieces = len(PIECES[gate])
-            if e + LOOKAHEAD < n_entries:
-                load_weight(e + LOOKAHEAD)
             if src == "p":
                 for k in range(n_pieces):
                     acc[k] = accs.tile([128, PIECES[gate][k][1]], F32, name="acc_%s%d" % (gate, k), tag="acc")

@@ -106,8 +106,9 @@ def tile_structuredlstmcell_w_kernel(
                 for g in range(ng):
                     nc.sync.dma_start(out=wt[:, g, 0:2048].bitcast(I32), in_=view[:, g, 0:512])
                 nc.sync.dma_start(out=wt[:, 0:2, 2048:4096].bitcast(I32), in_=view[:, 0:2, 512:1024])
-                nc.sync.dma_start(out=wt[:, 2:4, 2048:3072].bitcast(I32), in_=view[:, 2:4, 512:768])
-                nc.sync.dma_start(out=wt[:, 2:4, 3072:4096].bitcast(I32), in_=view[:, 2:4, 768:1024])
+                nc.sync.dma_start(out=wt[:, 2, 2048:4096].bitcast(I32), in_=view[:, 2, 512:1024])
+                nc.sync.dma_start(out=wt[:, 3, 2048:3072].bitcast(I32), in_=view[:, 3, 512:768])
+                nc.sync.dma_start(out=wt[:, 3, 3072:4096].bitcast(I32), in_=view[:, 3, 768:1024])
 
         for e in range(n_entries):
             if e == 1:
@@ -237,12 +238,9 @@ def tile_structuredlstmcell_w_kernel(
                 add_bias(gate, 0)
                 squash(gate, 0)
                 finish_h(0)
-                for g in range(2):
+                for g in range(4):
                     one_pass(e, g, 1)
                     one_pass(e, g, 2)
-                for k in (1, 2):
-                    one_pass(e, 2, k)
-                    one_pass(e, 3, k)
                 add_bias(gate, 1)
                 add_bias(gate, 2)
                 squash(gate, 1)

@@ -72,16 +72,23 @@ def tile_structuredlstmcell_w_kernel(
         nc.vector.memset(planes[:, 3:n_entries, :].bitcast(I32), 0)
         make_identity(nc, ident[:])
         plane_offset = []
+        small_loads = []
+        small_count = [0]
         for e in range(n_entries):
             scales = weights[stream[e]][1]
             ng = N_GROUPS[stream[e][0]]
             off = H_PLANE_OFFSET[stream[e][1]] if ng == 2 else 0
             plane_offset.append(off)
             for q in range(4):
-                nc.gpsimd.dma_start(
-                    out=planes[32 * q + off:32 * q + off + 4 * ng, e, :].bitcast(F32),
-                    in_=scales[:, 4 * q:4 * q + 4, :].bitcast(F32),
-                )
+                if ng == 4:
+                    nc.gpsimd.dma_start(
+                        out=planes[32 * q:32 * q + 16, e, :].bitcast(F32),
+                        in_=scales[:, 4 * q:4 * q + 4, :].bitcast(F32),
+                    )
+                else:
+                    for g in range(2):
+                        row = 32 * q + off + 4 * g
+                        small_loads.append((planes[row:row + 4, e, :].bitcast(I32), scales[g, 4 * q:4 * q + 4, :].bitcast(I32)))
         nc.scalar.activation(out=warm[:, 1:2], in_=warm[:, 0:1], func=ACT.Sigmoid)
 
         xs = keep.tile([128, K_ALL], BF16)
@@ -102,6 +109,10 @@ def tile_structuredlstmcell_w_kernel(
             if e < n_entries - 1:
                 for g in range(ng):
                     nc.sync.dma_start(out=wt[:, g, :].bitcast(I32), in_=view[:, g, :])
+                    if small_count[0] < len(small_loads):
+                        dst, rows = small_loads[small_count[0]]
+                        small_count[0] += 1
+                        nc.sync.dma_start(out=dst, in_=rows)
             else:
                 for g in range(ng):
                     nc.sync.dma_start(out=wt[:, g, 0:2048].bitcast(I32), in_=view[:, g, 0:512])

@@ -199,23 +199,22 @@ def tile_structuredlstmcell_w_kernel(
                 stop=(gx == 9),
             )
 
-        def add_bias(gate, k):
-            c0, w = PIECES[gate][k]
+        def add_bias(gate, k, c0, w):
             nc.vector.tensor_tensor(
-                out=acts[gate][:, c0:c0 + w], in0=acc[k][:],
+                out=acts[gate][:, c0:c0 + w], in0=acc[k][:, c0 - PIECES[gate][k][0]:c0 - PIECES[gate][k][0] + w],
                 in1=bias_sb[:, GATE_ROW[gate], c0:c0 + w], op=ALU.add,
             )
 
-        def squash(gate, k):
-            c0, w = PIECES[gate][k]
+        def squash(gate, c0, w):
             func = ACT.Tanh if gate == "g" else ACT.Sigmoid
             nc.scalar.activation(out=acts[gate][:, c0:c0 + w], in_=acts[gate][:, c0:c0 + w], func=func)
 
-        def finish_h(k):
-            c0, w = PIECES["o"][k]
+        def finish_h(c0, w):
             cols = slice(c0, c0 + w)
             nc.vector.tensor_tensor(out=acts["o"][:, cols], in0=acts["o"][:, cols], in1=tanh_c[:, cols], op=ALU.mult)
-            nc.sync.dma_start(out=out_0[:, cols], in_=acts["o"][:, cols])
+
+        def store_h(c0, w):
+            nc.sync.dma_start(out=out_0[:, c0:c0 + w], in_=acts["o"][:, c0:c0 + w])
 
         for e in range(n_entries):
             src, gate = stream[e]
@@ -223,8 +222,9 @@ def tile_structuredlstmcell_w_kernel(
             if src == "p":
                 for k in range(n_pieces):
                     acc[k] = accs.tile([128, PIECES[gate][k][1]], F32, name="acc_%s%d" % (gate, k), tag="acc")
-            if src == "x":
-                spread_bias(gate)
+            if e == 2:
+                for bias_gate in GATE_ORDER:
+                    spread_bias(bias_gate)
             if e < n_entries - 1:
                 for g in range(N_GROUPS[src]):
                     for k in range(n_pieces):
@@ -233,9 +233,9 @@ def tile_structuredlstmcell_w_kernel(
                 continue
             if gate != "o":
                 for k in range(n_pieces):
-                    add_bias(gate, k)
+                    add_bias(gate, k, *PIECES[gate][k])
                 for k in range(n_pieces):
-                    squash(gate, k)
+                    squash(gate, *PIECES[gate][k])
             if gate == "g":
                 nc.vector.tensor_tensor(out=acts["i"][:], in0=acts["i"][:], in1=acts["g"][:], op=ALU.mult)
             if gate == "f":
@@ -246,15 +246,18 @@ def tile_structuredlstmcell_w_kernel(
             if gate == "o":
                 for g in range(4):
                     one_pass(e, g, 0)
-                add_bias(gate, 0)
-                squash(gate, 0)
-                finish_h(0)
+                for c0 in (0, 256):
+                    add_bias(gate, 0, c0, 256)
+                    squash(gate, c0, 256)
+                for c0 in (0, 256):
+                    finish_h(c0, 256)
+                store_h(0, 512)
                 for g in range(4):
                     one_pass(e, g, 1)
                     one_pass(e, g, 2)
-                add_bias(gate, 1)
-                add_bias(gate, 2)
-                squash(gate, 1)
-                squash(gate, 2)
-                finish_h(1)
-                finish_h(2)
+                for k in (1, 2):
+                    add_bias(gate, k, *PIECES[gate][k])
+                    squash(gate, *PIECES[gate][k])
+                for k in (1, 2):
+                    finish_h(*PIECES[gate][k])
+                    store_h(*PIECES[gate][k])

from contextlib import ExitStack

import concourse.mybir as mybir
from concourse.masks import make_identity

F32 = mybir.dt.float32
BF16 = mybir.dt.bfloat16
U8 = mybir.dt.uint8
U32 = mybir.dt.uint32
I32 = mybir.dt.int32
FP8X4 = mybir.dt.float8_e4m3fn_x4
ACT = mybir.ActivationFunctionType
ALU = mybir.AluOpType

B = 128
H = 1024
HALF = 512
K_ALL = 5120
FLOPS = 2 * B * K_ALL * 4 * H

FIRST_GROUP = {"p": 0, "h": 4, "x": 6}
N_GROUPS = {"p": 4, "h": 2, "x": 4}
GATE_ORDER = "igfo"
GATE_ROW = {"i": 0, "f": 1, "g": 2, "o": 3}
H_PLANE_OFFSET = {"i": 0, "g": 8, "f": 0, "o": 8}
PIECES = {
    "i": [(0, 512), (512, 512)],
    "g": [(0, 512), (512, 512)],
    "f": [(0, 512), (512, 512)],
    "o": [(0, 512), (512, 256), (768, 256)],
}


def tile_structuredlstmcell_w_kernel(
    tc, P, hidden, cell, ext_input,
    W_pi_words, W_pi_scales, b_pi, W_pf_words, W_pf_scales, b_pf,
    W_pg_words, W_pg_scales, b_pg, W_po_words, W_po_scales, b_po,
    W_hi_words, W_hi_scales, W_hf_words, W_hf_scales,
    W_hg_words, W_hg_scales, W_ho_words, W_ho_scales,
    W_xi_words, W_xi_scales, W_xf_words, W_xf_scales,
    W_xg_words, W_xg_scales, W_xo_words, W_xo_scales,
    out_0, out_1,
):
    nc = tc.nc
    weights = {
        ("p", "i"): (W_pi_words, W_pi_scales), ("p", "f"): (W_pf_words, W_pf_scales),
        ("p", "g"): (W_pg_words, W_pg_scales), ("p", "o"): (W_po_words, W_po_scales),
        ("h", "i"): (W_hi_words, W_hi_scales), ("h", "f"): (W_hf_words, W_hf_scales),
        ("h", "g"): (W_hg_words, W_hg_scales), ("h", "o"): (W_ho_words, W_ho_scales),
        ("x", "i"): (W_xi_words, W_xi_scales), ("x", "f"): (W_xf_words, W_xf_scales),
        ("x", "g"): (W_xg_words, W_xg_scales), ("x", "o"): (W_xo_words, W_xo_scales),
    }
    biases = {"i": b_pi, "f": b_pf, "g": b_pg, "o": b_po}
    stream = [(src, gate) for gate in GATE_ORDER for src in "phx"]
    n_entries = len(stream)

    with ExitStack() as ctx:
        ctx.enter_context(tc.manual_schedule())
        keep = ctx.enter_context(tc.tile_pool(name="keep", bufs=1))
        wpool = ctx.enter_context(tc.tile_pool(name="wpool", bufs=1))
        prep = ctx.enter_context(tc.psum_pool(name="prep", bufs=3))
        accs = ctx.enter_context(tc.psum_pool(name="accs", bufs=5))

        planes = keep.tile([128, n_entries, H], U8, align_bytes=64)
        brow = keep.tile([128, H], BF16)
        ident = keep.tile([128, 128], F32)
        ident_bf = keep.tile([128, 128], BF16)
        warm = keep.tile([128, 2], F32)
        nc.vector.memset(planes[:, 0:3, :].bitcast(I32), 0)
        nc.vector.memset(warm[:], 0.0)
        nc.vector.memset(brow[:].bitcast(I32), 0)
        nc.vector.memset(planes[:, 3:n_entries, :].bitcast(I32), 0)
        make_identity(nc, ident[:])
        plane_offset = []
        small_loads = []
        small_count = [0]
        for e in range(n_entries):
            scales = weights[stream[e]][1]
            ng = N_GROUPS[stream[e][0]]
            off = H_PLANE_OFFSET[stream[e][1]] if ng == 2 else 0
            plane_offset.append(off)
            for q in range(4):
                if ng == 4:
                    nc.gpsimd.dma_start(
                        out=planes[32 * q:32 * q + 16, e, :].bitcast(F32),
                        in_=scales[:, 4 * q:4 * q + 4, :].bitcast(F32),
                    )
                else:
                    for g in range(2):
                        row = 32 * q + off + 4 * g
                        small_loads.append((planes[row:row + 4, e, :].bitcast(I32), scales[g, 4 * q:4 * q + 4, :].bitcast(I32)))
        nc.scalar.activation(out=warm[:, 1:2], in_=warm[:, 0:1], func=ACT.Sigmoid)

        xs = keep.tile([128, K_ALL], BF16)
        cell_sb = keep.tile([128, H], BF16)
        nc.sync.dma_start(out=xs[:, 0:2048], in_=P)
        nc.sync.dma_start(out=xs[:, 2048:3072], in_=hidden)
        nc.sync.dma_start(out=xs[:, 3072:5120], in_=ext_input)

        wtiles = {}

        def load_weight(e):
            src, gate = stream[e]
            words, scales = weights[(src, gate)]
            ng = N_GROUPS[src]
            wt = wpool.tile([128, ng, 4 * H], U8, name="w%d" % e, align_bytes=64)
            wtiles[e] = wt
            view = words.rearrange("g p n t -> p g (n t)").bitcast(I32)
            if e < n_entries - 1:
                for g in range(ng):
                    nc.sync.dma_start(out=wt[:, g, :].bitcast(I32), in_=view[:, g, :])
                    if small_count[0] < len(small_loads):
                        dst, rows = small_loads[small_count[0]]
                        small_count[0] += 1
                        nc.sync.dma_start(out=dst, in_=rows)
            else:
                for g in range(ng):
                    nc.sync.dma_start(out=wt[:, g, 0:2048].bitcast(I32), in_=view[:, g, 0:512])
                nc.sync.dma_start(out=wt[:, 0:2, 2048:4096].bitcast(I32), in_=view[:, 0:2, 512:1024])
                nc.sync.dma_start(out=wt[:, 2, 2048:4096].bitcast(I32), in_=view[:, 2, 512:1024])
                nc.sync.dma_start(out=wt[:, 3, 2048:3072].bitcast(I32), in_=view[:, 3, 512:768])
                nc.sync.dma_start(out=wt[:, 3, 3072:4096].bitcast(I32), in_=view[:, 3, 768:1024])

        for e in range(n_entries):
            if e == 1:
                for gate in "ifgo":
                    row = 32 * GATE_ROW[gate]
                    nc.scalar.dma_start(out=brow[row:row + 1, :], in_=biases[gate].rearrange("(o n) -> o n", o=1))
            if e == 6:
                nc.sync.dma_start(out=cell_sb[:], in_=cell)
            load_weight(e)

        grouped = keep.tile([128, 10, 128, 4], BF16, align_bytes=64)
        xcodes = keep.tile([128, 10 * 128], U32, align_bytes=64)
        xscales = keep.tile([128, 10 * 128], U8, align_bytes=64)
        xs_words = xs[:].bitcast(F32)
        grouped_words = grouped[:].bitcast(F32)

        def transpose_bank(j):
            xt = prep.tile([128, 2, 2, 128], F32, name="xt%d" % j, tag="prep")
            for gg in range(2):
                g = 2 * j + gg
                for u in range(2):
                    nc.tensor.transpose(xt[:, gg, u, :], xs_words[:, 256 * g + u:256 * (g + 1):2], ident[:])
            nc.vector.tensor_copy(
                out=grouped_words[:, 2 * j:2 * j + 2, :, :],
                in_=xt[:].rearrange("p g u b -> p g b u"),
            )

        def quantise(g0, g1):
            nc.vector.quantize_mx(
                out=xcodes[:, 128 * g0:128 * g1].bitcast(FP8X4),
                scales=xscales[:, 128 * g0:128 * g1],
                in_=grouped[:, g0:g1, :, :].rearrange("p g b t -> p (g b t)"),
            )

        for j in range(3):
            transpose_bank(j)
        quantise(0, 4)
        transpose_bank(3)
        quantise(4, 6)
        transpose_bank(4)
        nc.vector.tensor_copy(out=ident_bf[:], in_=ident[:])
        quantise(6, 10)

        bias_sb = keep.tile([128, 4, H], BF16)

        def spread_bias(gate):
            row = GATE_ROW[gate]
            for h in range(2):
                pb = prep.tile([128, HALF], F32, name="pb_%s%d" % (gate, h), tag="prep")
                nc.tensor.matmul(
                    out=pb[:],
                    lhsT=ident_bf[:, 32 * row:32 * row + 1].to_broadcast([128, 128]),
                    rhs=brow[:, HALF * h:HALF * (h + 1)],
                    start=True, stop=True,
                )
                nc.vector.tensor_copy(out=bias_sb[:, row, HALF * h:HALF * (h + 1)], in_=pb[:])

        acts = {}
        for gate in GATE_ORDER:
            acts[gate] = keep.tile([128, H], F32, name="act_" + gate)
        c_new = acts["f"]
        tanh_c = acts["g"]

        acc = {}

        def one_pass(e, g, k):
            src, gate = stream[e]
            c0, w = PIECES[gate][k]
            gx = FIRST_GROUP[src] + g
            nc.tensor.matmul_mx(
                out=acc[k][:],
                lhsT=xcodes[:, 128 * gx:128 * (gx + 1)].bitcast(FP8X4),
                lhsT_scale=xscales[:, 128 * gx:128 * (gx + 1)],
                rhs=wtiles[e][:, g, 4 * c0:4 * (c0 + w)].bitcast(FP8X4),
                rhs_scale=planes[plane_offset[e] + 4 * g:128, e, c0:c0 + w],
                start=(gx == 0),
                stop=(gx == 9),
            )

        def add_bias(gate, k, c0, w):
            nc.vector.tensor_tensor(
                out=acts[gate][:, c0:c0 + w], in0=acc[k][:, c0 - PIECES[gate][k][0]:c0 - PIECES[gate][k][0] + w],
                in1=bias_sb[:, GATE_ROW[gate], c0:c0 + w], op=ALU.add,
            )

        def squash(gate, c0, w):
            func = ACT.Tanh if gate == "g" else ACT.Sigmoid
            nc.scalar.activation(out=acts[gate][:, c0:c0 + w], in_=acts[gate][:, c0:c0 + w], func=func)

        def finish_h(c0, w):
            cols = slice(c0, c0 + w)
            nc.vector.tensor_tensor(out=acts["o"][:, cols], in0=acts["o"][:, cols], in1=tanh_c[:, cols], op=ALU.mult)

        def store_h(c0, w):
            nc.sync.dma_start(out=out_0[:, c0:c0 + w], in_=acts["o"][:, c0:c0 + w])

        for e in range(n_entries):
            src, gate = stream[e]
            n_pieces = len(PIECES[gate])
            if src == "p":
                for k in range(n_pieces):
                    acc[k] = accs.tile([128, PIECES[gate][k][1]], F32, name="acc_%s%d" % (gate, k), tag="acc")
            if e == 2:
                for bias_gate in GATE_ORDER:
                    spread_bias(bias_gate)
            if e < n_entries - 1:
                for g in range(N_GROUPS[src]):
                    for k in range(n_pieces):
                        one_pass(e, g, k)
            if src != "x":
                continue
            if gate != "o":
                for k in range(n_pieces):
                    add_bias(gate, k, *PIECES[gate][k])
                for k in range(n_pieces):
                    squash(gate, *PIECES[gate][k])
            if gate == "g":
                nc.vector.tensor_tensor(out=acts["i"][:], in0=acts["i"][:], in1=acts["g"][:], op=ALU.mult)
            if gate == "f":
                nc.vector.tensor_tensor(out=acts["f"][:], in0=acts["f"][:], in1=cell_sb[:], op=ALU.mult)
                nc.vector.tensor_tensor(out=c_new[:], in0=acts["f"][:], in1=acts["i"][:], op=ALU.add)
                nc.scalar.activation(out=tanh_c[:], in_=c_new[:], func=ACT.Tanh)
                nc.sync.dma_start(out=out_1, in_=c_new[:])
            if gate == "o":
                for g in range(4):
                    one_pass(e, g, 0)
                for c0 in (0, 256):
                    add_bias(gate, 0, c0, 256)
                    squash(gate, c0, 256)
                for c0 in (0, 256):
                    finish_h(c0, 256)
                store_h(0, 512)
                for g in range(4):
                    one_pass(e, g, 1)
                    one_pass(e, g, 2)
                for k in (1, 2):
                    add_bias(gate, k, *PIECES[gate][k])
                    squash(gate, *PIECES[gate][k])
                for k in (1, 2):
                    finish_h(*PIECES[gate][k])
                    store_h(*PIECES[gate][k])
